import numpy as np
import ml_dtypes

BF16 = ml_dtypes.bfloat16


def bf(x):
    return np.asarray(x, np.float32).astype(BF16)


def f32(x):
    return np.asarray(x, np.float32)


def f64(x):
    return np.asarray(x).astype(np.float64)


def striped(idx):
    return np.tile(idx.reshape(-1, 16).T, (8, 1))


C, H, DK, S, N, LK = 1024, 8, 128, 512, 128, 256
NEG = -1e9


def setup_inputs():
    return {
        "q": bf(np.random.standard_normal((C, N))),
        "k": bf(np.random.standard_normal((C, LK))),
        "v": bf(np.random.standard_normal((LK, C))),
        "bias": f32(np.random.standard_normal((H, N, LK))),
        "mask": f32(np.random.random((N, LK)) < 0.5),
        "bo": f32(0.1 * np.random.standard_normal((C, 1))),
        "base": f32(0.5 * np.random.standard_normal((C, S))),
        "offs": striped(np.random.permutation(S)[:N]),
    }


def reference(q, k, v, bias, mask, bo, base, offs):
    idx = offs[:16].T.reshape(-1)
    qh = f64(q).reshape(H, DK, N)
    kh = f64(k).reshape(H, DK, LK)
    vh = f64(v).reshape(LK, H, DK)
    s = np.einsum("hdn,hdt->hnt", qh, kh) / np.sqrt(DK) + f64(bias)
    s = np.where(f64(mask)[None] == 0.0, NEG, s)
    e = np.exp(s - s.max(axis=2, keepdims=True))
    a = e / e.sum(axis=2, keepdims=True)
    ctx = np.einsum("hnt,thd->hdn", a, vh).reshape(C, N)
    out = f64(base).copy()
    out[:, idx] = ctx + f64(bo)
    return out

@@ -1,0 +1,129 @@
+import math
+
+import concourse.mybir as mybir
+from concourse.masks import make_identity
+
+F32 = mybir.dt.float32
+BF16 = mybir.dt.bfloat16
+U16 = mybir.dt.uint16
+ALU = mybir.AluOpType
+ACT = mybir.ActivationFunctionType
+
+C, H, DK, S, N, LK = 1024, 8, 128, 512, 128, 256
+KEY_BLOCKS = LK // 128
+ROOT_DK = math.sqrt(DK)
+MASKED = -1.0e30
+
+FLOPS = 2 * H * N * LK * DK * 2
+
+
+def tile_powerlawattention_kernel(tc, q, k, v, bias, mask, bo, base, offs, out):
+    nc = tc.nc
+    with (
+        tc.tile_pool(name="held", bufs=1) as held,
+        tc.tile_pool(name="work", bufs=3) as work,
+        tc.tile_pool(name="stats", bufs=3) as stats,
+        tc.psum_pool(name="psum_scores", bufs=2) as psum_scores,
+        tc.psum_pool(name="psum_flip", bufs=2) as psum_flip,
+        tc.psum_pool(name="psum_ctx", bufs=2) as psum_ctx,
+        tc.psum_pool(name="psum_bo", bufs=1) as psum_bo,
+    ):
+        offsets = held.tile([128, N // 16], U16, name="offsets")
+        nc.sync.dma_start(offsets[:], offs)
+        mask_sb = held.tile([N, LK], F32, name="mask_sb")
+        nc.sync.dma_start(mask_sb[:], mask)
+
+        q_sb = held.tile([DK, H, N], BF16, name="q_sb")
+        k_sb = held.tile([DK, H, LK], BF16, name="k_sb")
+        bias_sb = held.tile([N, H, LK], F32, name="bias_sb")
+        v_sb = held.tile([128, KEY_BLOCKS, C], BF16, name="v_sb")
+        bo_rows = held.tile([H, DK], F32, name="bo_rows")
+        windows = [held.tile([DK, S], F32, name=f"window{h}") for h in range(H)]
+        q_heads = q.rearrange("(h d) n -> d h n", d=DK)
+        k_heads = k.rearrange("(h d) t -> d h t", d=DK)
+        bias_heads = bias.rearrange("h n t -> n h t")
+        for pair in range(H // 2):
+            two = slice(2 * pair, 2 * pair + 2)
+            nc.sync.dma_start(q_sb[:, two, :], q_heads[:, two, :])
+            nc.sync.dma_start(k_sb[:, two, :], k_heads[:, two, :])
+            nc.sync.dma_start(bias_sb[:, two, :], bias_heads[:, two, :])
+            if pair == 0:
+                nc.sync.dma_start(v_sb[:], v.rearrange("(c t) e -> t c e", t=128))
+                nc.sync.dma_start(bo_rows[:], bo.rearrange("(h d) o -> h (d o)", d=DK))
+            for h in (2 * pair, 2 * pair + 1):
+                nc.sync.dma_start(windows[h][:], base[h * DK : (h + 1) * DK, :])
+
+        ident_bf = held.tile([128, 128], BF16, name="ident_bf")
+        make_identity(nc, ident_bf[:])
+        ident_f32 = held.tile([128, 128], F32, name="ident_f32")
+        make_identity(nc, ident_f32[:])
+        ident_root = held.tile([128, 128], F32, name="ident_root")
+        nc.gpsimd.tensor_scalar_mul(ident_root[:], ident_f32[:], ROOT_DK)
+
+        scratch = held.tile([128, 1], F32, name="scratch")
+        nc.vector.memset(scratch[:], 0.0)
+        nc.scalar.activation(scratch[:], scratch[:], ACT.Exp)
+
+        mask_term = held.tile([N, 2, LK], BF16, name="mask_term")
+        nc.vector.tensor_scalar(
+            mask_term[:], mask_sb[:].unsqueeze(1).to_broadcast([N, 2, LK]), -MASKED, MASKED, ALU.mult, ALU.add
+        )
+
+        bo_ps = psum_bo.tile([DK, H], F32, name="bo_ps")
+        nc.tensor.matmul(bo_ps[:], lhsT=bo_rows[:], rhs=ident_f32[0:H, 0:H], start=True, stop=True)
+        bo_sb = held.tile([DK, H], F32, name="bo_sb")
+        nc.vector.tensor_copy(bo_sb[:], bo_ps[:])
+        bo_wide = held.tile([DK, H, N], F32, name="bo_wide")
+        nc.gpsimd.tensor_copy(bo_wide[:], bo_sb[:].unsqueeze(2).to_broadcast([DK, H, N]))
+
+        for pair in range(H // 2):
+            two = slice(2 * pair, 2 * pair + 2)
+            scores = psum_scores.tile([N, 2, LK], F32)
+            nc.tensor.matmul(scores[:], lhsT=ident_bf[:], rhs=mask_term[:], start=True, stop=False)
+            for j in range(2):
+                h = 2 * pair + j
+                nc.tensor.matmul(scores[:, j, :], lhsT=q_sb[:, h, :], rhs=k_sb[:, h, :], start=False, stop=False)
+            nc.tensor.matmul(scores[:], lhsT=ident_root[:], rhs=bias_sb[:, two, :], start=False, stop=True)
+
+            top = stats.tile([N, 2], F32)
+            nc.vector.reduce_max(top[:], scores[:], axis=mybir.AxisListType.X)
+            shift = stats.tile([N, 2], F32)
+            nc.vector.tensor_scalar_mul(shift[:], top[:], -1.0 / ROOT_DK)
+
+            grown = work.tile([N, 2, LK], F32)
+            total = stats.tile([N, 2], F32)
+            for j in range(2):
+                nc.scalar.activation(
+                    grown[:, j, :],
+                    scores[:, j, :],
+                    ACT.Exp,
+                    bias=shift[:, j : j + 1],
+                    scale=1.0 / ROOT_DK,
+                    accum_out=total[:, j : j + 1],
+                )
+            inverse = stats.tile([N, 2], F32)
+            nc.vector.reciprocal(inverse[:], total[:])
+
+            for j in range(2):
+                h = 2 * pair + j
+                weights = work.tile([N, LK], BF16)
+                nc.scalar.activation(weights[:], grown[:, j, :], ACT.Copy, scale=inverse[:, j : j + 1])
+                flipped_ps = psum_flip.tile([128, KEY_BLOCKS, N], BF16)
+                for c in range(KEY_BLOCKS):
+                    nc.tensor.transpose(flipped_ps[:, c, :], weights[:, c * 128 : (c + 1) * 128], ident_bf[:])
+                flipped = work.tile([128, KEY_BLOCKS, N], BF16)
+                nc.scalar.copy(flipped[:], flipped_ps[:])
+
+                ctx_ps = psum_ctx.tile([DK, N], F32)
+                for c in range(KEY_BLOCKS):
+                    nc.tensor.matmul(
+                        ctx_ps[:],
+                        lhsT=v_sb[:, c, h * DK : (h + 1) * DK],
+                        rhs=flipped[:, c, :],
+                        start=(c == 0),
+                        stop=(c == KEY_BLOCKS - 1),
+                    )
+                ctx = work.tile([DK, N], F32)
+                nc.scalar.copy(ctx[:], ctx_ps[:])
+                nc.vector.tensor_tensor(windows[h][:].indirect(offsets[:]), ctx[:], bo_wide[:, h, :], ALU.add)
+                nc.sync.dma_start(out[h * DK : (h + 1) * DK, :], windows[h][:])

@@ -10,9 +10,10 @@ ALU = mybir.AluOpType
 ACT = mybir.ActivationFunctionType
 
 C, H, DK, S, N, LK = 1024, 8, 128, 512, 128, 256
+PAIRS = H // 2
 KEY_BLOCKS = LK // 128
-ROOT_DK = math.sqrt(DK)
 MASKED = -1.0e30
+WARMING_MATMULS = 3
 
 FLOPS = 2 * H * N * LK * DK * 2
 
@@ -21,8 +22,8 @@ def tile_powerlawattention_kernel(tc, q, k, v, bias, mask, bo, base, offs, out):
     nc = tc.nc
     with (
         tc.tile_pool(name="held", bufs=1) as held,
-        tc.tile_pool(name="work", bufs=3) as work,
-        tc.tile_pool(name="stats", bufs=3) as stats,
+        tc.tile_pool(name="per_pair", bufs=PAIRS) as per_pair,
+        tc.tile_pool(name="per_head", bufs=4) as per_head,
         tc.psum_pool(name="psum_scores", bufs=2) as psum_scores,
         tc.psum_pool(name="psum_flip", bufs=2) as psum_flip,
         tc.psum_pool(name="psum_ctx", bufs=2) as psum_ctx,
@@ -30,35 +31,32 @@ def tile_powerlawattention_kernel(tc, q, k, v, bias, mask, bo, base, offs, out):
     ):
         offsets = held.tile([128, N // 16], U16, name="offsets")
         nc.sync.dma_start(offsets[:], offs)
+        bo_rows = held.tile([H, DK], F32, name="bo_rows")
+        nc.sync.dma_start(bo_rows[:], bo.rearrange("(h d) o -> h (d o)", d=DK))
         mask_sb = held.tile([N, LK], F32, name="mask_sb")
         nc.sync.dma_start(mask_sb[:], mask)
 
         q_sb = held.tile([DK, H, N], BF16, name="q_sb")
         k_sb = held.tile([DK, H, LK], BF16, name="k_sb")
         bias_sb = held.tile([N, H, LK], F32, name="bias_sb")
-        v_sb = held.tile([128, KEY_BLOCKS, C], BF16, name="v_sb")
-        bo_rows = held.tile([H, DK], F32, name="bo_rows")
-        windows = [held.tile([DK, S], F32, name=f"window{h}") for h in range(H)]
         q_heads = q.rearrange("(h d) n -> d h n", d=DK)
         k_heads = k.rearrange("(h d) t -> d h t", d=DK)
         bias_heads = bias.rearrange("h n t -> n h t")
-        for pair in range(H // 2):
+        for pair in range(PAIRS):
             two = slice(2 * pair, 2 * pair + 2)
             nc.sync.dma_start(q_sb[:, two, :], q_heads[:, two, :])
             nc.sync.dma_start(k_sb[:, two, :], k_heads[:, two, :])
             nc.sync.dma_start(bias_sb[:, two, :], bias_heads[:, two, :])
-            if pair == 0:
-                nc.sync.dma_start(v_sb[:], v.rearrange("(c t) e -> t c e", t=128))
-                nc.sync.dma_start(bo_rows[:], bo.rearrange("(h d) o -> h (d o)", d=DK))
-            for h in (2 * pair, 2 * pair + 1):
-                nc.sync.dma_start(windows[h][:], base[h * DK : (h + 1) * DK, :])
+        v_sb = held.tile([128, KEY_BLOCKS, C], BF16, name="v_sb")
+        nc.sync.dma_start(v_sb[:], v.rearrange("(c t) e -> t c e", t=128))
+        windows = [held.tile([DK, S], F32, name=f"window{h}") for h in range(H)]
+        for h in range(H):
+            nc.sync.dma_start(windows[h][:], base[h * DK : (h + 1) * DK, :])
 
         ident_bf = held.tile([128, 128], BF16, name="ident_bf")
         make_identity(nc, ident_bf[:])
-        ident_f32 = held.tile([128, 128], F32, name="ident_f32")
-        make_identity(nc, ident_f32[:])
-        ident_root = held.tile([128, 128], F32, name="ident_root")
-        nc.gpsimd.tensor_scalar_mul(ident_root[:], ident_f32[:], ROOT_DK)
+        ident_h = held.tile([H, H], F32, name="ident_h")
+        make_identity(nc, ident_h[:])
 
         scratch = held.tile([128, 1], F32, name="scratch")
         nc.vector.memset(scratch[:], 0.0)
@@ -69,49 +67,54 @@ def tile_powerlawattention_kernel(tc, q, k, v, bias, mask, bo, base, offs, out):
             mask_term[:], mask_sb[:].unsqueeze(1).to_broadcast([N, 2, LK]), -MASKED, MASKED, ALU.mult, ALU.add
         )
 
-        bo_ps = psum_bo.tile([DK, H], F32, name="bo_ps")
-        nc.tensor.matmul(bo_ps[:], lhsT=bo_rows[:], rhs=ident_f32[0:H, 0:H], start=True, stop=True)
+        zeros = held.tile([128, 512], BF16, name="zeros")
+        nc.vector.memset(zeros[:], 0.0)
+        spare_ps = psum_bo.tile([128, 512], F32, name="spare_ps")
+        for i in range(WARMING_MATMULS):
+            nc.tensor.matmul(spare_ps[:], lhsT=zeros[:, 0:128], rhs=zeros[:], start=True, stop=True)
+
+        nc.tensor.matmul(spare_ps[:, 0:H], lhsT=bo_rows[:], rhs=ident_h[:], start=True, stop=True)
         bo_sb = held.tile([DK, H], F32, name="bo_sb")
-        nc.vector.tensor_copy(bo_sb[:], bo_ps[:])
+        nc.vector.tensor_copy(bo_sb[:], spare_ps[:, 0:H])
         bo_wide = held.tile([DK, H, N], F32, name="bo_wide")
         nc.gpsimd.tensor_copy(bo_wide[:], bo_sb[:].unsqueeze(2).to_broadcast([DK, H, N]))
 
-        for pair in range(H // 2):
+        for pair in range(PAIRS):
             two = slice(2 * pair, 2 * pair + 2)
-            scores = psum_scores.tile([N, 2, LK], F32)
-            nc.tensor.matmul(scores[:], lhsT=ident_bf[:], rhs=mask_term[:], start=True, stop=False)
+            products = psum_scores.tile([N, 2, LK], F32)
             for j in range(2):
                 h = 2 * pair + j
-                nc.tensor.matmul(scores[:, j, :], lhsT=q_sb[:, h, :], rhs=k_sb[:, h, :], start=False, stop=False)
-            nc.tensor.matmul(scores[:], lhsT=ident_root[:], rhs=bias_sb[:, two, :], start=False, stop=True)
+                nc.tensor.matmul(products[:, j, :], lhsT=q_sb[:, h, :], rhs=k_sb[:, h, :], start=(j == 0), stop=False)
+            nc.tensor.matmul(products[:], lhsT=ident_bf[:], rhs=mask_term[:], start=False, stop=True)
 
-            top = stats.tile([N, 2], F32)
-            nc.vector.reduce_max(top[:], scores[:], axis=mybir.AxisListType.X)
-            shift = stats.tile([N, 2], F32)
-            nc.vector.tensor_scalar_mul(shift[:], top[:], -1.0 / ROOT_DK)
+            scores = per_pair.tile([N, 2, LK], F32)
+            nc.vector.scalar_tensor_tensor(
+                scores[:], products[:], 1.0 / math.sqrt(DK), bias_sb[:, two, :], ALU.mult, ALU.add
+            )
+            minus_top = per_pair.tile([N, 2], F32)
+            nc.vector.reduce_max(minus_top[:], scores[:], axis=mybir.AxisListType.X, negate=True)
 
-            grown = work.tile([N, 2, LK], F32)
-            total = stats.tile([N, 2], F32)
+            total = per_pair.tile([N, 2], F32)
             for j in range(2):
                 nc.scalar.activation(
-                    grown[:, j, :],
+                    scores[:, j, :],
                     scores[:, j, :],
                     ACT.Exp,
-                    bias=shift[:, j : j + 1],
-                    scale=1.0 / ROOT_DK,
+                    bias=minus_top[:, j : j + 1],
                     accum_out=total[:, j : j + 1],
                 )
-            inverse = stats.tile([N, 2], F32)
+            inverse = per_pair.tile([N, 2], F32)
             nc.vector.reciprocal(inverse[:], total[:])
 
             for j in range(2):
                 h = 2 * pair + j
-                weights = work.tile([N, LK], BF16)
-                nc.scalar.activation(weights[:], grown[:, j, :], ACT.Copy, scale=inverse[:, j : j + 1])
+                weights = per_head.tile([N, LK], BF16)
+                nc.gpsimd.tensor_scalar(weights[:], scores[:, j, :], inverse[:, j : j + 1], 0.0, ALU.mult, ALU.add)
+
                 flipped_ps = psum_flip.tile([128, KEY_BLOCKS, N], BF16)
                 for c in range(KEY_BLOCKS):
                     nc.tensor.transpose(flipped_ps[:, c, :], weights[:, c * 128 : (c + 1) * 128], ident_bf[:])
-                flipped = work.tile([128, KEY_BLOCKS, N], BF16)
+                flipped = per_head.tile([128, KEY_BLOCKS, N], BF16)
                 nc.scalar.copy(flipped[:], flipped_ps[:])
 
                 ctx_ps = psum_ctx.tile([DK, N], F32)
@@ -123,7 +126,7 @@ def tile_powerlawattention_kernel(tc, q, k, v, bias, mask, bo, base, offs, out):
                         start=(c == 0),
                         stop=(c == KEY_BLOCKS - 1),
                     )
-                ctx = work.tile([DK, N], F32)
+                ctx = per_head.tile([DK, N], F32)
                 nc.scalar.copy(ctx[:], ctx_ps[:])
                 nc.vector.tensor_tensor(windows[h][:].indirect(offsets[:]), ctx[:], bo_wide[:, h, :], ALU.add)
                 nc.sync.dma_start(out[h * DK : (h + 1) * DK, :], windows[h][:])

@@ -27,29 +27,29 @@ def tile_powerlawattention_kernel(tc, q, k, v, bias, mask, bo, base, offs, out):
         tc.psum_pool(name="psum_scores", bufs=2) as psum_scores,
         tc.psum_pool(name="psum_flip", bufs=2) as psum_flip,
         tc.psum_pool(name="psum_ctx", bufs=2) as psum_ctx,
-        tc.psum_pool(name="psum_bo", bufs=1) as psum_bo,
+        tc.psum_pool(name="psum_spare", bufs=1) as psum_spare,
     ):
-        offsets = held.tile([128, N // 16], U16, name="offsets")
-        nc.sync.dma_start(offsets[:], offs)
-        bo_rows = held.tile([H, DK], F32, name="bo_rows")
-        nc.sync.dma_start(bo_rows[:], bo.rearrange("(h d) o -> h (d o)", d=DK))
         mask_sb = held.tile([N, LK], F32, name="mask_sb")
-        nc.sync.dma_start(mask_sb[:], mask)
-
         q_sb = held.tile([DK, H, N], BF16, name="q_sb")
         k_sb = held.tile([DK, H, LK], BF16, name="k_sb")
         bias_sb = held.tile([N, H, LK], F32, name="bias_sb")
+        v_sb = held.tile([128, KEY_BLOCKS, C], BF16, name="v_sb")
+        bo_rows = held.tile([H, DK], F32, name="bo_rows")
+        offsets = held.tile([128, N // 16], U16, name="offsets")
+        windows = [held.tile([DK, S], F32, name=f"window{h}") for h in range(H)]
         q_heads = q.rearrange("(h d) n -> d h n", d=DK)
         k_heads = k.rearrange("(h d) t -> d h t", d=DK)
         bias_heads = bias.rearrange("h n t -> n h t")
+
+        nc.scalar.dma_start(bo_rows[:], bo.rearrange("(h d) o -> h (d o)", d=DK))
+        nc.sync.dma_start(mask_sb[:], mask)
         for pair in range(PAIRS):
             two = slice(2 * pair, 2 * pair + 2)
+            nc.scalar.dma_start(k_sb[:, two, :], k_heads[:, two, :])
             nc.sync.dma_start(q_sb[:, two, :], q_heads[:, two, :])
-            nc.sync.dma_start(k_sb[:, two, :], k_heads[:, two, :])
             nc.sync.dma_start(bias_sb[:, two, :], bias_heads[:, two, :])
-        v_sb = held.tile([128, KEY_BLOCKS, C], BF16, name="v_sb")
-        nc.sync.dma_start(v_sb[:], v.rearrange("(c t) e -> t c e", t=128))
-        windows = [held.tile([DK, S], F32, name=f"window{h}") for h in range(H)]
+        nc.scalar.dma_start(v_sb[:], v.rearrange("(c t) e -> t c e", t=128))
+        nc.sync.dma_start(offsets[:], offs)
         for h in range(H):
             nc.sync.dma_start(windows[h][:], base[h * DK : (h + 1) * DK, :])
 
@@ -62,16 +62,14 @@ def tile_powerlawattention_kernel(tc, q, k, v, bias, mask, bo, base, offs, out):
         nc.vector.memset(scratch[:], 0.0)
         nc.scalar.activation(scratch[:], scratch[:], ACT.Exp)
 
-        mask_term = held.tile([N, 2, LK], BF16, name="mask_term")
-        nc.vector.tensor_scalar(
-            mask_term[:], mask_sb[:].unsqueeze(1).to_broadcast([N, 2, LK]), -MASKED, MASKED, ALU.mult, ALU.add
-        )
-
         zeros = held.tile([128, 512], BF16, name="zeros")
         nc.vector.memset(zeros[:], 0.0)
-        spare_ps = psum_bo.tile([128, 512], F32, name="spare_ps")
+        spare_ps = psum_spare.tile([128, 512], F32, name="spare_ps")
         for i in range(WARMING_MATMULS):
             nc.tensor.matmul(spare_ps[:], lhsT=zeros[:, 0:128], rhs=zeros[:], start=True, stop=True)
+
+        mask_term = held.tile([N, LK], BF16, name="mask_term")
+        nc.vector.tensor_scalar(mask_term[:], mask_sb[:], -MASKED, MASKED, ALU.mult, ALU.add)
 
         nc.tensor.matmul(spare_ps[:, 0:H], lhsT=bo_rows[:], rhs=ident_h[:], start=True, stop=True)
         bo_sb = held.tile([DK, H], F32, name="bo_sb")
@@ -79,13 +77,20 @@ def tile_powerlawattention_kernel(tc, q, k, v, bias, mask, bo, base, offs, out):
         bo_wide = held.tile([DK, H, N], F32, name="bo_wide")
         nc.gpsimd.tensor_copy(bo_wide[:], bo_sb[:].unsqueeze(2).to_broadcast([DK, H, N]))
 
+        ctx = [held.tile([DK, N], F32, name=f"ctx{h}") for h in range(H)]
         for pair in range(PAIRS):
             two = slice(2 * pair, 2 * pair + 2)
             products = psum_scores.tile([N, 2, LK], F32)
             for j in range(2):
                 h = 2 * pair + j
                 nc.tensor.matmul(products[:, j, :], lhsT=q_sb[:, h, :], rhs=k_sb[:, h, :], start=(j == 0), stop=False)
-            nc.tensor.matmul(products[:], lhsT=ident_bf[:], rhs=mask_term[:], start=False, stop=True)
+            nc.tensor.matmul(
+                products[:],
+                lhsT=ident_bf[:],
+                rhs=mask_term[:].unsqueeze(1).to_broadcast([N, 2, LK]),
+                start=False,
+                stop=True,
+            )
 
             scores = per_pair.tile([N, 2, LK], F32)
             nc.vector.scalar_tensor_tensor(
@@ -126,7 +131,8 @@ def tile_powerlawattention_kernel(tc, q, k, v, bias, mask, bo, base, offs, out):
                         start=(c == 0),
                         stop=(c == KEY_BLOCKS - 1),
                     )
-                ctx = per_head.tile([DK, N], F32)
-                nc.scalar.copy(ctx[:], ctx_ps[:])
-                nc.vector.tensor_tensor(windows[h][:].indirect(offsets[:]), ctx[:], bo_wide[:, h, :], ALU.add)
-                nc.sync.dma_start(out[h * DK : (h + 1) * DK, :], windows[h][:])
+                nc.scalar.copy(ctx[h][:], ctx_ps[:])
+
+        for h in range(H):
+            nc.vector.tensor_tensor(windows[h][:].indirect(offsets[:]), ctx[h][:], bo_wide[:, h, :], ALU.add)
+            nc.sync.dma_start(out[h * DK : (h + 1) * DK, :], windows[h][:])

@@ -27,29 +27,29 @@ def tile_powerlawattention_kernel(tc, q, k, v, bias, mask, bo, base, offs, out):
         tc.psum_pool(name="psum_scores", bufs=2) as psum_scores,
         tc.psum_pool(name="psum_flip", bufs=2) as psum_flip,
         tc.psum_pool(name="psum_ctx", bufs=2) as psum_ctx,
-        tc.psum_pool(name="psum_spare", bufs=1) as psum_spare,
+        tc.psum_pool(name="psum_bo", bufs=1) as psum_bo,
     ):
+        offsets = held.tile([128, N // 16], U16, name="offsets")
+        nc.sync.dma_start(offsets[:], offs)
+        bo_rows = held.tile([H, DK], F32, name="bo_rows")
+        nc.sync.dma_start(bo_rows[:], bo.rearrange("(h d) o -> h (d o)", d=DK))
         mask_sb = held.tile([N, LK], F32, name="mask_sb")
+        nc.sync.dma_start(mask_sb[:], mask)
+
         q_sb = held.tile([DK, H, N], BF16, name="q_sb")
         k_sb = held.tile([DK, H, LK], BF16, name="k_sb")
         bias_sb = held.tile([N, H, LK], F32, name="bias_sb")
-        v_sb = held.tile([128, KEY_BLOCKS, C], BF16, name="v_sb")
-        bo_rows = held.tile([H, DK], F32, name="bo_rows")
-        offsets = held.tile([128, N // 16], U16, name="offsets")
-        windows = [held.tile([DK, S], F32, name=f"window{h}") for h in range(H)]
         q_heads = q.rearrange("(h d) n -> d h n", d=DK)
         k_heads = k.rearrange("(h d) t -> d h t", d=DK)
         bias_heads = bias.rearrange("h n t -> n h t")
-
-        nc.scalar.dma_start(bo_rows[:], bo.rearrange("(h d) o -> h (d o)", d=DK))
-        nc.sync.dma_start(mask_sb[:], mask)
         for pair in range(PAIRS):
             two = slice(2 * pair, 2 * pair + 2)
-            nc.scalar.dma_start(k_sb[:, two, :], k_heads[:, two, :])
             nc.sync.dma_start(q_sb[:, two, :], q_heads[:, two, :])
+            nc.sync.dma_start(k_sb[:, two, :], k_heads[:, two, :])
             nc.sync.dma_start(bias_sb[:, two, :], bias_heads[:, two, :])
-        nc.scalar.dma_start(v_sb[:], v.rearrange("(c t) e -> t c e", t=128))
-        nc.sync.dma_start(offsets[:], offs)
+        v_sb = held.tile([128, KEY_BLOCKS, C], BF16, name="v_sb")
+        nc.sync.dma_start(v_sb[:], v.rearrange("(c t) e -> t c e", t=128))
+        windows = [held.tile([DK, S], F32, name=f"window{h}") for h in range(H)]
         for h in range(H):
             nc.sync.dma_start(windows[h][:], base[h * DK : (h + 1) * DK, :])
 
@@ -62,14 +62,16 @@ def tile_powerlawattention_kernel(tc, q, k, v, bias, mask, bo, base, offs, out):
         nc.vector.memset(scratch[:], 0.0)
         nc.scalar.activation(scratch[:], scratch[:], ACT.Exp)
 
+        mask_term = held.tile([N, 2, LK], BF16, name="mask_term")
+        nc.vector.tensor_scalar(
+            mask_term[:], mask_sb[:].unsqueeze(1).to_broadcast([N, 2, LK]), -MASKED, MASKED, ALU.mult, ALU.add
+        )
+
         zeros = held.tile([128, 512], BF16, name="zeros")
         nc.vector.memset(zeros[:], 0.0)
-        spare_ps = psum_spare.tile([128, 512], F32, name="spare_ps")
+        spare_ps = psum_bo.tile([128, 512], F32, name="spare_ps")
         for i in range(WARMING_MATMULS):
             nc.tensor.matmul(spare_ps[:], lhsT=zeros[:, 0:128], rhs=zeros[:], start=True, stop=True)
-
-        mask_term = held.tile([N, LK], BF16, name="mask_term")
-        nc.vector.tensor_scalar(mask_term[:], mask_sb[:], -MASKED, MASKED, ALU.mult, ALU.add)
 
         nc.tensor.matmul(spare_ps[:, 0:H], lhsT=bo_rows[:], rhs=ident_h[:], start=True, stop=True)
         bo_sb = held.tile([DK, H], F32, name="bo_sb")
@@ -77,20 +79,13 @@ def tile_powerlawattention_kernel(tc, q, k, v, bias, mask, bo, base, offs, out):
         bo_wide = held.tile([DK, H, N], F32, name="bo_wide")
         nc.gpsimd.tensor_copy(bo_wide[:], bo_sb[:].unsqueeze(2).to_broadcast([DK, H, N]))
 
-        ctx = [held.tile([DK, N], F32, name=f"ctx{h}") for h in range(H)]
         for pair in range(PAIRS):
             two = slice(2 * pair, 2 * pair + 2)
             products = psum_scores.tile([N, 2, LK], F32)
             for j in range(2):
                 h = 2 * pair + j
                 nc.tensor.matmul(products[:, j, :], lhsT=q_sb[:, h, :], rhs=k_sb[:, h, :], start=(j == 0), stop=False)
-            nc.tensor.matmul(
-                products[:],
-                lhsT=ident_bf[:],
-                rhs=mask_term[:].unsqueeze(1).to_broadcast([N, 2, LK]),
-                start=False,
-                stop=True,
-            )
+            nc.tensor.matmul(products[:], lhsT=ident_bf[:], rhs=mask_term[:], start=False, stop=True)
 
             scores = per_pair.tile([N, 2, LK], F32)
             nc.vector.scalar_tensor_tensor(
@@ -114,7 +109,7 @@ def tile_powerlawattention_kernel(tc, q, k, v, bias, mask, bo, base, offs, out):
             for j in range(2):
                 h = 2 * pair + j
                 weights = per_head.tile([N, LK], BF16)
-                nc.gpsimd.tensor_scalar(weights[:], scores[:, j, :], inverse[:, j : j + 1], 0.0, ALU.mult, ALU.add)
+                nc.scalar.activation(weights[:], scores[:, j, :], ACT.Copy, scale=inverse[:, j : j + 1])
 
                 flipped_ps = psum_flip.tile([128, KEY_BLOCKS, N], BF16)
                 for c in range(KEY_BLOCKS):
@@ -131,8 +126,7 @@ def tile_powerlawattention_kernel(tc, q, k, v, bias, mask, bo, base, offs, out):
                         start=(c == 0),
                         stop=(c == KEY_BLOCKS - 1),
                     )
-                nc.scalar.copy(ctx[h][:], ctx_ps[:])
-
-        for h in range(H):
-            nc.vector.tensor_tensor(windows[h][:].indirect(offsets[:]), ctx[h][:], bo_wide[:, h, :], ALU.add)
-            nc.sync.dma_start(out[h * DK : (h + 1) * DK, :], windows[h][:])
+                ctx = per_head.tile([DK, N], F32)
+                nc.scalar.copy(ctx[:], ctx_ps[:])
+                nc.vector.tensor_tensor(windows[h][:].indirect(offsets[:]), ctx[:], bo_wide[:, h, :], ALU.add)
+                nc.sync.dma_start(out[h * DK : (h + 1) * DK, :], windows[h][:])

@@ -10,7 +10,6 @@ ALU = mybir.AluOpType
 ACT = mybir.ActivationFunctionType
 
 C, H, DK, S, N, LK = 1024, 8, 128, 512, 128, 256
-PAIRS = H // 2
 KEY_BLOCKS = LK // 128
 MASKED = -1.0e30
 WARMING_MATMULS = 3
@@ -22,12 +21,11 @@ def tile_powerlawattention_kernel(tc, q, k, v, bias, mask, bo, base, offs, out):
     nc = tc.nc
     with (
         tc.tile_pool(name="held", bufs=1) as held,
-        tc.tile_pool(name="per_pair", bufs=PAIRS) as per_pair,
-        tc.tile_pool(name="per_head", bufs=4) as per_head,
-        tc.psum_pool(name="psum_scores", bufs=2) as psum_scores,
+        tc.tile_pool(name="work", bufs=4) as work,
+        tc.psum_pool(name="psum_products", bufs=3) as psum_products,
         tc.psum_pool(name="psum_flip", bufs=2) as psum_flip,
         tc.psum_pool(name="psum_ctx", bufs=2) as psum_ctx,
-        tc.psum_pool(name="psum_bo", bufs=1) as psum_bo,
+        tc.psum_pool(name="psum_spare", bufs=1) as psum_spare,
     ):
         offsets = held.tile([128, N // 16], U16, name="offsets")
         nc.sync.dma_start(offsets[:], offs)
@@ -42,8 +40,8 @@ def tile_powerlawattention_kernel(tc, q, k, v, bias, mask, bo, base, offs, out):
         q_heads = q.rearrange("(h d) n -> d h n", d=DK)
         k_heads = k.rearrange("(h d) t -> d h t", d=DK)
         bias_heads = bias.rearrange("h n t -> n h t")
-        for pair in range(PAIRS):
-            two = slice(2 * pair, 2 * pair + 2)
+        for first in range(0, H, 2):
+            two = slice(first, first + 2)
             nc.sync.dma_start(q_sb[:, two, :], q_heads[:, two, :])
             nc.sync.dma_start(k_sb[:, two, :], k_heads[:, two, :])
             nc.sync.dma_start(bias_sb[:, two, :], bias_heads[:, two, :])
@@ -62,14 +60,12 @@ def tile_powerlawattention_kernel(tc, q, k, v, bias, mask, bo, base, offs, out):
         nc.vector.memset(scratch[:], 0.0)
         nc.scalar.activation(scratch[:], scratch[:], ACT.Exp)
 
-        mask_term = held.tile([N, 2, LK], BF16, name="mask_term")
-        nc.vector.tensor_scalar(
-            mask_term[:], mask_sb[:].unsqueeze(1).to_broadcast([N, 2, LK]), -MASKED, MASKED, ALU.mult, ALU.add
-        )
+        mask_term = held.tile([N, LK], BF16, name="mask_term")
+        nc.vector.tensor_scalar(mask_term[:], mask_sb[:], -MASKED, MASKED, ALU.mult, ALU.add)
 
         zeros = held.tile([128, 512], BF16, name="zeros")
         nc.vector.memset(zeros[:], 0.0)
-        spare_ps = psum_bo.tile([128, 512], F32, name="spare_ps")
+        spare_ps = psum_spare.tile([128, 512], F32, name="spare_ps")
         for i in range(WARMING_MATMULS):
             nc.tensor.matmul(spare_ps[:], lhsT=zeros[:, 0:128], rhs=zeros[:], start=True, stop=True)
 
@@ -79,54 +75,42 @@ def tile_powerlawattention_kernel(tc, q, k, v, bias, mask, bo, base, offs, out):
         bo_wide = held.tile([DK, H, N], F32, name="bo_wide")
         nc.gpsimd.tensor_copy(bo_wide[:], bo_sb[:].unsqueeze(2).to_broadcast([DK, H, N]))
 
-        for pair in range(PAIRS):
-            two = slice(2 * pair, 2 * pair + 2)
-            products = psum_scores.tile([N, 2, LK], F32)
-            for j in range(2):
-                h = 2 * pair + j
-                nc.tensor.matmul(products[:, j, :], lhsT=q_sb[:, h, :], rhs=k_sb[:, h, :], start=(j == 0), stop=False)
+        ctx = [held.tile([DK, N], F32, name=f"ctx{h}") for h in range(H)]
+        for h in range(H):
+            products = psum_products.tile([N, LK], F32)
+            nc.tensor.matmul(products[:], lhsT=q_sb[:, h, :], rhs=k_sb[:, h, :], start=True, stop=False)
             nc.tensor.matmul(products[:], lhsT=ident_bf[:], rhs=mask_term[:], start=False, stop=True)
 
-            scores = per_pair.tile([N, 2, LK], F32)
+            scores = work.tile([N, LK], F32)
             nc.vector.scalar_tensor_tensor(
-                scores[:], products[:], 1.0 / math.sqrt(DK), bias_sb[:, two, :], ALU.mult, ALU.add
+                scores[:], products[:], 1.0 / math.sqrt(DK), bias_sb[:, h, :], ALU.mult, ALU.add
             )
-            minus_top = per_pair.tile([N, 2], F32)
+            minus_top = work.tile([N, 1], F32)
             nc.vector.reduce_max(minus_top[:], scores[:], axis=mybir.AxisListType.X, negate=True)
-
-            total = per_pair.tile([N, 2], F32)
-            for j in range(2):
-                nc.scalar.activation(
-                    scores[:, j, :],
-                    scores[:, j, :],
-                    ACT.Exp,
-                    bias=minus_top[:, j : j + 1],
-                    accum_out=total[:, j : j + 1],
-                )
-            inverse = per_pair.tile([N, 2], F32)
+            total = work.tile([N, 1], F32)
+            nc.scalar.activation(scores[:], scores[:], ACT.Exp, bias=minus_top[:], accum_out=total[:])
+            inverse = work.tile([N, 1], F32)
             nc.vector.reciprocal(inverse[:], total[:])
+            weights = work.tile([N, LK], BF16)
+            nc.scalar.activation(weights[:], scores[:], ACT.Copy, scale=inverse[:])
 
-            for j in range(2):
-                h = 2 * pair + j
-                weights = per_head.tile([N, LK], BF16)
-                nc.scalar.activation(weights[:], scores[:, j, :], ACT.Copy, scale=inverse[:, j : j + 1])
+            flipped_ps = psum_flip.tile([128, KEY_BLOCKS, N], BF16)
+            for c in range(KEY_BLOCKS):
+                nc.tensor.transpose(flipped_ps[:, c, :], weights[:, c * 128 : (c + 1) * 128], ident_bf[:])
+            flipped = work.tile([128, KEY_BLOCKS, N], BF16)
+            nc.scalar.copy(flipped[:], flipped_ps[:])
 
-                flipped_ps = psum_flip.tile([128, KEY_BLOCKS, N], BF16)
-                for c in range(KEY_BLOCKS):
-                    nc.tensor.transpose(flipped_ps[:, c, :], weights[:, c * 128 : (c + 1) * 128], ident_bf[:])
-                flipped = per_head.tile([128, KEY_BLOCKS, N], BF16)
-                nc.scalar.copy(flipped[:], flipped_ps[:])
+            ctx_ps = psum_ctx.tile([DK, N], F32)
+            for c in range(KEY_BLOCKS):
+                nc.tensor.matmul(
+                    ctx_ps[:],
+                    lhsT=v_sb[:, c, h * DK : (h + 1) * DK],
+                    rhs=flipped[:, c, :],
+                    start=(c == 0),
+                    stop=(c == KEY_BLOCKS - 1),
+                )
+            nc.scalar.copy(ctx[h][:], ctx_ps[:])
 
-                ctx_ps = psum_ctx.tile([DK, N], F32)
-                for c in range(KEY_BLOCKS):
-                    nc.tensor.matmul(
-                        ctx_ps[:],
-                        lhsT=v_sb[:, c, h * DK : (h + 1) * DK],
-                        rhs=flipped[:, c, :],
-                        start=(c == 0),
-                        stop=(c == KEY_BLOCKS - 1),
-                    )
-                ctx = per_head.tile([DK, N], F32)
-                nc.scalar.copy(ctx[:], ctx_ps[:])
-                nc.vector.tensor_tensor(windows[h][:].indirect(offsets[:]), ctx[:], bo_wide[:, h, :], ALU.add)
-                nc.sync.dma_start(out[h * DK : (h + 1) * DK, :], windows[h][:])
+        for h in range(H):
+            nc.vector.tensor_tensor(windows[h][:].indirect(offsets[:]), ctx[h][:], bo_wide[:, h, :], ALU.add)
+            nc.sync.dma_start(out[h * DK : (h + 1) * DK, :], windows[h][:])

@@ -96,7 +96,9 @@ def tile_powerlawattention_kernel(tc, q, k, v, bias, mask, bo, base, offs, out):
 
             flipped_ps = psum_flip.tile([128, KEY_BLOCKS, N], BF16)
             for c in range(KEY_BLOCKS):
-                nc.tensor.transpose(flipped_ps[:, c, :], weights[:, c * 128 : (c + 1) * 128], ident_bf[:])
+                nc.tensor.matmul(
+                    flipped_ps[:, c, :], lhsT=weights[:, c * 128 : (c + 1) * 128], rhs=ident_bf[:], start=True, stop=True
+                )
             flipped = work.tile([128, KEY_BLOCKS, N], BF16)
             nc.scalar.copy(flipped[:], flipped_ps[:])
 

@@ -21,7 +21,7 @@ def tile_powerlawattention_kernel(tc, q, k, v, bias, mask, bo, base, offs, out):
     nc = tc.nc
     with (
         tc.tile_pool(name="held", bufs=1) as held,
-        tc.tile_pool(name="work", bufs=4) as work,
+        tc.tile_pool(name="work", bufs=H) as work,
         tc.psum_pool(name="psum_products", bufs=3) as psum_products,
         tc.psum_pool(name="psum_flip", bufs=2) as psum_flip,
         tc.psum_pool(name="psum_ctx", bufs=2) as psum_ctx,

@@ -70,10 +70,8 @@ def tile_powerlawattention_kernel(tc, q, k, v, bias, mask, bo, base, offs, out):
             nc.tensor.matmul(spare_ps[:], lhsT=zeros[:, 0:128], rhs=zeros[:], start=True, stop=True)
 
         nc.tensor.matmul(spare_ps[:, 0:H], lhsT=bo_rows[:], rhs=ident_h[:], start=True, stop=True)
-        bo_sb = held.tile([DK, H], F32, name="bo_sb")
-        nc.vector.tensor_copy(bo_sb[:], spare_ps[:, 0:H])
         bo_wide = held.tile([DK, H, N], F32, name="bo_wide")
-        nc.gpsimd.tensor_copy(bo_wide[:], bo_sb[:].unsqueeze(2).to_broadcast([DK, H, N]))
+        nc.scalar.copy(bo_wide[:], spare_ps[:, 0:H].unsqueeze(2).to_broadcast([DK, H, N]))
 
         ctx = [held.tile([DK, N], F32, name=f"ctx{h}") for h in range(H)]
         for h in range(H):

@@ -22,10 +22,10 @@ def tile_powerlawattention_kernel(tc, q, k, v, bias, mask, bo, base, offs, out):
     with (
         tc.tile_pool(name="held", bufs=1) as held,
         tc.tile_pool(name="work", bufs=H) as work,
-        tc.psum_pool(name="psum_products", bufs=3) as psum_products,
+        tc.psum_pool(name="psum_products", bufs=2) as psum_products,
         tc.psum_pool(name="psum_flip", bufs=2) as psum_flip,
+        tc.psum_pool(name="psum_rows", bufs=2) as psum_rows,
         tc.psum_pool(name="psum_ctx", bufs=2) as psum_ctx,
-        tc.psum_pool(name="psum_spare", bufs=1) as psum_spare,
     ):
         offsets = held.tile([128, N // 16], U16, name="offsets")
         nc.sync.dma_start(offsets[:], offs)
@@ -53,8 +53,8 @@ def tile_powerlawattention_kernel(tc, q, k, v, bias, mask, bo, base, offs, out):
 
         ident_bf = held.tile([128, 128], BF16, name="ident_bf")
         make_identity(nc, ident_bf[:])
-        ident_h = held.tile([H, H], F32, name="ident_h")
-        make_identity(nc, ident_h[:])
+        ident_f = held.tile([128, 128], F32, name="ident_f")
+        make_identity(nc, ident_f[:])
 
         scratch = held.tile([128, 1], F32, name="scratch")
         nc.vector.memset(scratch[:], 0.0)
@@ -65,11 +65,11 @@ def tile_powerlawattention_kernel(tc, q, k, v, bias, mask, bo, base, offs, out):
 
         zeros = held.tile([128, 512], BF16, name="zeros")
         nc.vector.memset(zeros[:], 0.0)
-        spare_ps = psum_spare.tile([128, 512], F32, name="spare_ps")
+        spare_ps = psum_products.tile([128, 512], F32, name="spare_ps", tag="products")
         for i in range(WARMING_MATMULS):
             nc.tensor.matmul(spare_ps[:], lhsT=zeros[:, 0:128], rhs=zeros[:], start=True, stop=True)
 
-        nc.tensor.matmul(spare_ps[:, 0:H], lhsT=bo_rows[:], rhs=ident_h[:], start=True, stop=True)
+        nc.tensor.matmul(spare_ps[:, 0:H], lhsT=bo_rows[:], rhs=ident_f[0:H, 0:H], start=True, stop=True)
         bo_wide = held.tile([DK, H, N], F32, name="bo_wide")
         nc.scalar.copy(bo_wide[:], spare_ps[:, 0:H].unsqueeze(2).to_broadcast([DK, H, N]))
 
@@ -85,12 +85,11 @@ def tile_powerlawattention_kernel(tc, q, k, v, bias, mask, bo, base, offs, out):
             )
             minus_top = work.tile([N, 1], F32)
             nc.vector.reduce_max(minus_top[:], scores[:], axis=mybir.AxisListType.X, negate=True)
+            weights = work.tile([N, LK], BF16)
             total = work.tile([N, 1], F32)
-            nc.scalar.activation(scores[:], scores[:], ACT.Exp, bias=minus_top[:], accum_out=total[:])
+            nc.scalar.activation(weights[:], scores[:], ACT.Exp, bias=minus_top[:], accum_out=total[:])
             inverse = work.tile([N, 1], F32)
             nc.vector.reciprocal(inverse[:], total[:])
-            weights = work.tile([N, LK], BF16)
-            nc.scalar.activation(weights[:], scores[:], ACT.Copy, scale=inverse[:])
 
             flipped_ps = psum_flip.tile([128, KEY_BLOCKS, N], BF16)
             for c in range(KEY_BLOCKS):
@@ -100,15 +99,19 @@ def tile_powerlawattention_kernel(tc, q, k, v, bias, mask, bo, base, offs, out):
             flipped = work.tile([128, KEY_BLOCKS, N], BF16)
             nc.scalar.copy(flipped[:], flipped_ps[:])
 
-            ctx_ps = psum_ctx.tile([DK, N], F32)
+            rows_ps = psum_rows.tile([N, DK], F32)
             for c in range(KEY_BLOCKS):
                 nc.tensor.matmul(
-                    ctx_ps[:],
-                    lhsT=v_sb[:, c, h * DK : (h + 1) * DK],
-                    rhs=flipped[:, c, :],
+                    rows_ps[:],
+                    lhsT=flipped[:, c, :],
+                    rhs=v_sb[:, c, h * DK : (h + 1) * DK],
                     start=(c == 0),
                     stop=(c == KEY_BLOCKS - 1),
                 )
+            rows = work.tile([N, DK], F32)
+            nc.scalar.activation(rows[:], rows_ps[:], ACT.Copy, scale=inverse[:])
+            ctx_ps = psum_ctx.tile([DK, N], F32)
+            nc.tensor.transpose(ctx_ps[:], rows[:], ident_f[:])
             nc.scalar.copy(ctx[h][:], ctx_ps[:])
 
         for h in range(H):

@@ -22,10 +22,10 @@ def tile_powerlawattention_kernel(tc, q, k, v, bias, mask, bo, base, offs, out):
     with (
         tc.tile_pool(name="held", bufs=1) as held,
         tc.tile_pool(name="work", bufs=H) as work,
-        tc.psum_pool(name="psum_products", bufs=2) as psum_products,
+        tc.psum_pool(name="psum_products", bufs=3) as psum_products,
         tc.psum_pool(name="psum_flip", bufs=2) as psum_flip,
         tc.psum_pool(name="psum_rows", bufs=2) as psum_rows,
-        tc.psum_pool(name="psum_ctx", bufs=2) as psum_ctx,
+        tc.psum_pool(name="psum_ctx", bufs=1) as psum_ctx,
     ):
         offsets = held.tile([128, N // 16], U16, name="offsets")
         nc.sync.dma_start(offsets[:], offs)

@@ -12,7 +12,6 @@ ACT = mybir.ActivationFunctionType
 C, H, DK, S, N, LK = 1024, 8, 128, 512, 128, 256
 KEY_BLOCKS = LK // 128
 MASKED = -1.0e30
-WARMING_MATMULS = 3
 
 FLOPS = 2 * H * N * LK * DK * 2
 
@@ -40,16 +39,29 @@ def tile_powerlawattention_kernel(tc, q, k, v, bias, mask, bo, base, offs, out):
         q_heads = q.rearrange("(h d) n -> d h n", d=DK)
         k_heads = k.rearrange("(h d) t -> d h t", d=DK)
         bias_heads = bias.rearrange("h n t -> n h t")
-        for first in range(0, H, 2):
-            two = slice(first, first + 2)
+        v_sb = [held.tile([128, KEY_BLOCKS, C // 2], BF16, name=f"v_sb{half}") for half in range(2)]
+        v_halves = v.rearrange("(c t) (half e) -> half t c e", t=128, half=2)
+        windows = [held.tile([DK, S], F32, name=f"window{h}") for h in range(H)]
+
+        def load_scores_of_pair(j):
+            two = slice(2 * j, 2 * j + 2)
             nc.sync.dma_start(q_sb[:, two, :], q_heads[:, two, :])
             nc.sync.dma_start(k_sb[:, two, :], k_heads[:, two, :])
             nc.sync.dma_start(bias_sb[:, two, :], bias_heads[:, two, :])
-        v_sb = held.tile([128, KEY_BLOCKS, C], BF16, name="v_sb")
-        nc.sync.dma_start(v_sb[:], v.rearrange("(c t) e -> t c e", t=128))
-        windows = [held.tile([DK, S], F32, name=f"window{h}") for h in range(H)]
-        for h in range(H):
+
+        def load_window(h):
             nc.sync.dma_start(windows[h][:], base[h * DK : (h + 1) * DK, :])
+
+        load_scores_of_pair(0)
+        load_scores_of_pair(1)
+        nc.sync.dma_start(v_sb[0][:], v_halves[0])
+        load_scores_of_pair(2)
+        load_window(0)
+        load_scores_of_pair(3)
+        load_window(1)
+        nc.sync.dma_start(v_sb[1][:], v_halves[1])
+        for h in range(2, H):
+            load_window(h)
 
         ident_bf = held.tile([128, 128], BF16, name="ident_bf")
         make_identity(nc, ident_bf[:])
@@ -63,12 +75,7 @@ def tile_powerlawattention_kernel(tc, q, k, v, bias, mask, bo, base, offs, out):
         mask_term = held.tile([N, LK], BF16, name="mask_term")
         nc.vector.tensor_scalar(mask_term[:], mask_sb[:], -MASKED, MASKED, ALU.mult, ALU.add)
 
-        zeros = held.tile([128, 512], BF16, name="zeros")
-        nc.vector.memset(zeros[:], 0.0)
         spare_ps = psum_products.tile([128, 512], F32, name="spare_ps", tag="products")
-        for i in range(WARMING_MATMULS):
-            nc.tensor.matmul(spare_ps[:], lhsT=zeros[:, 0:128], rhs=zeros[:], start=True, stop=True)
-
         nc.tensor.matmul(spare_ps[:, 0:H], lhsT=bo_rows[:], rhs=ident_f[0:H, 0:H], start=True, stop=True)
         bo_wide = held.tile([DK, H, N], F32, name="bo_wide")
         nc.scalar.copy(bo_wide[:], spare_ps[:, 0:H].unsqueeze(2).to_broadcast([DK, H, N]))
@@ -104,7 +111,7 @@ def tile_powerlawattention_kernel(tc, q, k, v, bias, mask, bo, base, offs, out):
                 nc.tensor.matmul(
                     rows_ps[:],
                     lhsT=flipped[:, c, :],
-                    rhs=v_sb[:, c, h * DK : (h + 1) * DK],
+                    rhs=v_sb[h // 4][:, c, (h % 4) * DK : (h % 4 + 1) * DK],
                     start=(c == 0),
                     stop=(c == KEY_BLOCKS - 1),
                 )

@@ -12,6 +12,7 @@ ACT = mybir.ActivationFunctionType
 C, H, DK, S, N, LK = 1024, 8, 128, 512, 128, 256
 KEY_BLOCKS = LK // 128
 MASKED = -1.0e30
+WARMING_MATMULS = 5
 
 FLOPS = 2 * H * N * LK * DK * 2
 
@@ -27,41 +28,55 @@ def tile_powerlawattention_kernel(tc, q, k, v, bias, mask, bo, base, offs, out):
         tc.psum_pool(name="psum_ctx", bufs=1) as psum_ctx,
     ):
         offsets = held.tile([128, N // 16], U16, name="offsets")
-        nc.sync.dma_start(offsets[:], offs)
         bo_rows = held.tile([H, DK], F32, name="bo_rows")
-        nc.sync.dma_start(bo_rows[:], bo.rearrange("(h d) o -> h (d o)", d=DK))
         mask_sb = held.tile([N, LK], F32, name="mask_sb")
-        nc.sync.dma_start(mask_sb[:], mask)
-
         q_sb = held.tile([DK, H, N], BF16, name="q_sb")
         k_sb = held.tile([DK, H, LK], BF16, name="k_sb")
         bias_sb = held.tile([N, H, LK], F32, name="bias_sb")
+        v_sb = [held.tile([128, KEY_BLOCKS, C // 2], BF16, name=f"v_sb{half}") for half in range(2)]
+        windows = [held.tile([DK, S], F32, name=f"window{h}") for h in range(H)]
         q_heads = q.rearrange("(h d) n -> d h n", d=DK)
         k_heads = k.rearrange("(h d) t -> d h t", d=DK)
         bias_heads = bias.rearrange("h n t -> n h t")
-        v_sb = [held.tile([128, KEY_BLOCKS, C // 2], BF16, name=f"v_sb{half}") for half in range(2)]
         v_halves = v.rearrange("(c t) (half e) -> half t c e", t=128, half=2)
-        windows = [held.tile([DK, S], F32, name=f"window{h}") for h in range(H)]
 
-        def load_scores_of_pair(j):
-            two = slice(2 * j, 2 * j + 2)
-            nc.sync.dma_start(q_sb[:, two, :], q_heads[:, two, :])
-            nc.sync.dma_start(k_sb[:, two, :], k_heads[:, two, :])
-            nc.sync.dma_start(bias_sb[:, two, :], bias_heads[:, two, :])
+        def load_q_and_k(first, last):
+            heads = slice(first, last + 1)
+            nc.sync.dma_start(q_sb[:, heads, :], q_heads[:, heads, :])
+            nc.sync.dma_start(k_sb[:, heads, :], k_heads[:, heads, :])
+
+        def load_bias(first, last):
+            heads = slice(first, last + 1)
+            nc.sync.dma_start(bias_sb[:, heads, :], bias_heads[:, heads, :])
+
+        def load_v(half):
+            nc.sync.dma_start(v_sb[half][:], v_halves[half])
 
         def load_window(h):
             nc.sync.dma_start(windows[h][:], base[h * DK : (h + 1) * DK, :])
 
-        load_scores_of_pair(0)
-        load_scores_of_pair(1)
-        nc.sync.dma_start(v_sb[0][:], v_halves[0])
-        load_scores_of_pair(2)
+        nc.sync.dma_start(bo_rows[:], bo.rearrange("(h d) o -> h (d o)", d=DK))
+        nc.sync.dma_start(mask_sb[:], mask)
+        load_q_and_k(0, 0)
+        load_bias(0, 0)
+        load_q_and_k(1, 3)
+        load_bias(1, 1)
+        load_bias(2, 3)
+        nc.sync.dma_start(offsets[:], offs)
+        load_q_and_k(4, 7)
+        load_bias(4, 5)
+        load_v(0)
+        load_bias(6, 7)
         load_window(0)
-        load_scores_of_pair(3)
-        load_window(1)
-        nc.sync.dma_start(v_sb[1][:], v_halves[1])
-        for h in range(2, H):
+        load_v(1)
+        for h in range(1, H):
             load_window(h)
+
+        zeros = held.tile([128, 256], BF16, name="zeros")
+        nc.vector.memset(zeros[:], 0.0)
+        spare_ps = psum_ctx.tile([128, 256], F32, name="spare_ps", tag="ctx_ps")
+        for i in range(WARMING_MATMULS):
+            nc.tensor.matmul(spare_ps[:, 0:256], lhsT=zeros[:, 0:128], rhs=zeros[:], start=True, stop=True)
 
         ident_bf = held.tile([128, 128], BF16, name="ident_bf")
         make_identity(nc, ident_bf[:])
@@ -75,16 +90,17 @@ def tile_powerlawattention_kernel(tc, q, k, v, bias, mask, bo, base, offs, out):
         mask_term = held.tile([N, LK], BF16, name="mask_term")
         nc.vector.tensor_scalar(mask_term[:], mask_sb[:], -MASKED, MASKED, ALU.mult, ALU.add)
 
-        spare_ps = psum_products.tile([128, 512], F32, name="spare_ps", tag="products")
-        nc.tensor.matmul(spare_ps[:, 0:H], lhsT=bo_rows[:], rhs=ident_f[0:H, 0:H], start=True, stop=True)
-        bo_wide = held.tile([DK, H, N], F32, name="bo_wide")
-        nc.scalar.copy(bo_wide[:], spare_ps[:, 0:H].unsqueeze(2).to_broadcast([DK, H, N]))
-
         ctx = [held.tile([DK, N], F32, name=f"ctx{h}") for h in range(H)]
         for h in range(H):
+            if h == 1:
+                bo_ps = psum_products.tile([DK, H], F32, name="bo_ps", tag="products")
+                nc.tensor.matmul(bo_ps[:], lhsT=bo_rows[:], rhs=ident_f[0:H, 0:H], start=True, stop=True)
+                bo_columns = held.tile([DK, H], F32, name="bo_columns")
+                nc.scalar.copy(bo_columns[:], bo_ps[:])
+
             products = psum_products.tile([N, LK], F32)
-            nc.tensor.matmul(products[:], lhsT=q_sb[:, h, :], rhs=k_sb[:, h, :], start=True, stop=False)
-            nc.tensor.matmul(products[:], lhsT=ident_bf[:], rhs=mask_term[:], start=False, stop=True)
+            nc.tensor.matmul(products[:], lhsT=ident_bf[:], rhs=mask_term[:], start=True, stop=False)
+            nc.tensor.matmul(products[:], lhsT=q_sb[:, h, :], rhs=k_sb[:, h, :], start=False, stop=True)
 
             scores = work.tile([N, LK], F32)
             nc.vector.scalar_tensor_tensor(
@@ -121,6 +137,10 @@ def tile_powerlawattention_kernel(tc, q, k, v, bias, mask, bo, base, offs, out):
             nc.tensor.transpose(ctx_ps[:], rows[:], ident_f[:])
             nc.scalar.copy(ctx[h][:], ctx_ps[:])
 
+        bo_wide = held.tile([DK, H, N], F32, name="bo_wide")
         for h in range(H):
+            if h % 2 == 0:
+                two = slice(h, h + 2)
+                nc.scalar.copy(bo_wide[:, two, :], bo_columns[:, two].unsqueeze(2).to_broadcast([DK, 2, N]))
             nc.vector.tensor_tensor(windows[h][:].indirect(offsets[:]), ctx[h][:], bo_wide[:, h, :], ALU.add)
             nc.sync.dma_start(out[h * DK : (h + 1) * DK, :], windows[h][:])

@@ -12,7 +12,7 @@ ACT = mybir.ActivationFunctionType
 C, H, DK, S, N, LK = 1024, 8, 128, 512, 128, 256
 KEY_BLOCKS = LK // 128
 MASKED = -1.0e30
-WARMING_MATMULS = 5
+WARMING_MATMULS = 8
 
 FLOPS = 2 * H * N * LK * DK * 2
 

@@ -10,6 +10,7 @@ ALU = mybir.AluOpType
 ACT = mybir.ActivationFunctionType
 
 C, H, DK, S, N, LK = 1024, 8, 128, 512, 128, 256
+PAIRS = H // 2
 KEY_BLOCKS = LK // 128
 MASKED = -1.0e30
 WARMING_MATMULS = 8
@@ -30,46 +31,45 @@ def tile_powerlawattention_kernel(tc, q, k, v, bias, mask, bo, base, offs, out):
         offsets = held.tile([128, N // 16], U16, name="offsets")
         bo_rows = held.tile([H, DK], F32, name="bo_rows")
         mask_sb = held.tile([N, LK], F32, name="mask_sb")
-        q_sb = held.tile([DK, H, N], BF16, name="q_sb")
-        k_sb = held.tile([DK, H, LK], BF16, name="k_sb")
+        q_sb = held.tile([128, PAIRS, 2, N], BF16, name="q_sb")
+        k_sb = held.tile([128, PAIRS, 2, LK], BF16, name="k_sb")
         bias_sb = held.tile([N, H, LK], F32, name="bias_sb")
-        v_sb = [held.tile([128, KEY_BLOCKS, C // 2], BF16, name=f"v_sb{half}") for half in range(2)]
+        v_sb = held.tile([128, KEY_BLOCKS, C], BF16, name="v_sb")
         windows = [held.tile([DK, S], F32, name=f"window{h}") for h in range(H)]
-        q_heads = q.rearrange("(h d) n -> d h n", d=DK)
-        k_heads = k.rearrange("(h d) t -> d h t", d=DK)
+        q_pairs = q.rearrange("(j p two) n -> p j (two n)", p=128, two=2)
+        k_pairs = k.rearrange("(j p two) t -> p j (two t)", p=128, two=2)
         bias_heads = bias.rearrange("h n t -> n h t")
-        v_halves = v.rearrange("(c t) (half e) -> half t c e", t=128, half=2)
 
-        def load_q_and_k(first, last):
-            heads = slice(first, last + 1)
-            nc.sync.dma_start(q_sb[:, heads, :], q_heads[:, heads, :])
-            nc.sync.dma_start(k_sb[:, heads, :], k_heads[:, heads, :])
+        def load_q(first, last):
+            pairs = slice(first, last + 1)
+            nc.sync.dma_start(q_sb[:, pairs, :, :].rearrange("p j two n -> p j (two n)"), q_pairs[:, pairs, :])
+
+        def load_k(j):
+            nc.sync.dma_start(k_sb[:, j, :, :].rearrange("p two t -> p (two t)"), k_pairs[:, j, :])
 
         def load_bias(first, last):
             heads = slice(first, last + 1)
             nc.sync.dma_start(bias_sb[:, heads, :], bias_heads[:, heads, :])
 
-        def load_v(half):
-            nc.sync.dma_start(v_sb[half][:], v_halves[half])
-
         def load_window(h):
             nc.sync.dma_start(windows[h][:], base[h * DK : (h + 1) * DK, :])
 
-        nc.sync.dma_start(bo_rows[:], bo.rearrange("(h d) o -> h (d o)", d=DK))
+        load_q(0, 0)
         nc.sync.dma_start(mask_sb[:], mask)
-        load_q_and_k(0, 0)
+        load_k(0)
+        nc.sync.dma_start(bo_rows[:], bo.rearrange("(h d) o -> h (d o)", d=DK))
         load_bias(0, 0)
-        load_q_and_k(1, 3)
         load_bias(1, 1)
+        load_q(1, PAIRS - 1)
+        load_k(1)
         load_bias(2, 3)
         nc.sync.dma_start(offsets[:], offs)
-        load_q_and_k(4, 7)
+        load_k(2)
         load_bias(4, 5)
-        load_v(0)
+        nc.sync.dma_start(v_sb[:], v.rearrange("(c t) e -> t c e", t=128))
+        load_k(3)
         load_bias(6, 7)
-        load_window(0)
-        load_v(1)
-        for h in range(1, H):
+        for h in range(H):
             load_window(h)
 
         zeros = held.tile([128, 256], BF16, name="zeros")
@@ -82,6 +82,19 @@ def tile_powerlawattention_kernel(tc, q, k, v, bias, mask, bo, base, offs, out):
         make_identity(nc, ident_bf[:])
         ident_f = held.tile([128, 128], F32, name="ident_f")
         make_identity(nc, ident_f[:])
+
+        q_own = [held.tile([128, PAIRS, 2, N], BF16, name=f"q_own{x}") for x in range(2)]
+        own = [slice(64 * x, 64 * (x + 1)) for x in range(2)]
+        for x in range(2):
+            nc.vector.memset(q_own[x][own[1 - x], 0, :, :], 0.0)
+            nc.vector.tensor_copy(q_own[x][own[x], 0, :, :], q_sb[own[x], 0, :, :])
+        for x in range(2):
+            nc.gpsimd.memset(q_own[x][own[1 - x], 1:PAIRS, :, :], 0.0)
+        for j in range(1, PAIRS):
+            for x in range(2):
+                nc.gpsimd.tensor_scalar(
+                    q_own[x][own[x], j, :, :], q_sb[own[x], j, :, :], 1.0, 0.0, ALU.mult, ALU.add
+                )
 
         scratch = held.tile([128, 1], F32, name="scratch")
         nc.vector.memset(scratch[:], 0.0)
@@ -100,7 +113,11 @@ def tile_powerlawattention_kernel(tc, q, k, v, bias, mask, bo, base, offs, out):
 
             products = psum_products.tile([N, LK], F32)
             nc.tensor.matmul(products[:], lhsT=ident_bf[:], rhs=mask_term[:], start=True, stop=False)
-            nc.tensor.matmul(products[:], lhsT=q_sb[:, h, :], rhs=k_sb[:, h, :], start=False, stop=True)
+            j, x = divmod(h, 2)
+            for two in range(2):
+                nc.tensor.matmul(
+                    products[:], lhsT=q_own[x][:, j, two, :], rhs=k_sb[:, j, two, :], start=False, stop=(two == 1)
+                )
 
             scores = work.tile([N, LK], F32)
             nc.vector.scalar_tensor_tensor(
@@ -127,7 +144,7 @@ def tile_powerlawattention_kernel(tc, q, k, v, bias, mask, bo, base, offs, out):
                 nc.tensor.matmul(
                     rows_ps[:],
                     lhsT=flipped[:, c, :],
-                    rhs=v_sb[h // 4][:, c, (h % 4) * DK : (h % 4 + 1) * DK],
+                    rhs=v_sb[:, c, h * DK : (h + 1) * DK],
                     start=(c == 0),
                     stop=(c == KEY_BLOCKS - 1),
                 )

import math

import concourse.mybir as mybir
from concourse.masks import make_identity

F32 = mybir.dt.float32
BF16 = mybir.dt.bfloat16
U16 = mybir.dt.uint16
ALU = mybir.AluOpType
ACT = mybir.ActivationFunctionType

C, H, DK, S, N, LK = 1024, 8, 128, 512, 128, 256
PAIRS = H // 2
KEY_BLOCKS = LK // 128
MASKED = -1.0e30
WARMING_MATMULS = 8

FLOPS = 2 * H * N * LK * DK * 2


def tile_powerlawattention_kernel(tc, q, k, v, bias, mask, bo, base, offs, out):
    nc = tc.nc
    with (
        tc.tile_pool(name="held", bufs=1) as held,
        tc.tile_pool(name="work", bufs=H) as work,
        tc.psum_pool(name="psum_products", bufs=3) as psum_products,
        tc.psum_pool(name="psum_flip", bufs=2) as psum_flip,
        tc.psum_pool(name="psum_rows", bufs=2) as psum_rows,
        tc.psum_pool(name="psum_ctx", bufs=1) as psum_ctx,
    ):
        offsets = held.tile([128, N // 16], U16, name="offsets")
        bo_rows = held.tile([H, DK], F32, name="bo_rows")
        mask_sb = held.tile([N, LK], F32, name="mask_sb")
        q_sb = held.tile([128, PAIRS, 2, N], BF16, name="q_sb")
        k_sb = held.tile([128, PAIRS, 2, LK], BF16, name="k_sb")
        bias_sb = held.tile([N, H, LK], F32, name="bias_sb")
        v_sb = held.tile([128, KEY_BLOCKS, C], BF16, name="v_sb")
        windows = [held.tile([DK, S], F32, name=f"window{h}") for h in range(H)]
        q_pairs = q.rearrange("(j p two) n -> p j (two n)", p=128, two=2)
        k_pairs = k.rearrange("(j p two) t -> p j (two t)", p=128, two=2)
        bias_heads = bias.rearrange("h n t -> n h t")

        def load_q(first, last):
            pairs = slice(first, last + 1)
            nc.sync.dma_start(q_sb[:, pairs, :, :].rearrange("p j two n -> p j (two n)"), q_pairs[:, pairs, :])

        def load_k(j):
            nc.sync.dma_start(k_sb[:, j, :, :].rearrange("p two t -> p (two t)"), k_pairs[:, j, :])

        def load_bias(first, last):
            heads = slice(first, last + 1)
            nc.sync.dma_start(bias_sb[:, heads, :], bias_heads[:, heads, :])

        def load_window(h):
            nc.sync.dma_start(windows[h][:], base[h * DK : (h + 1) * DK, :])

        load_q(0, 0)
        nc.sync.dma_start(mask_sb[:], mask)
        load_k(0)
        nc.sync.dma_start(bo_rows[:], bo.rearrange("(h d) o -> h (d o)", d=DK))
        load_bias(0, 0)
        load_bias(1, 1)
        load_q(1, PAIRS - 1)
        load_k(1)
        load_bias(2, 3)
        nc.sync.dma_start(offsets[:], offs)
        load_k(2)
        load_bias(4, 5)
        nc.sync.dma_start(v_sb[:], v.rearrange("(c t) e -> t c e", t=128))
        load_k(3)
        load_bias(6, 7)
        for h in range(H):
            load_window(h)

        zeros = held.tile([128, 256], BF16, name="zeros")
        nc.vector.memset(zeros[:], 0.0)
        spare_ps = psum_ctx.tile([128, 256], F32, name="spare_ps", tag="ctx_ps")
        for i in range(WARMING_MATMULS):
            nc.tensor.matmul(spare_ps[:, 0:256], lhsT=zeros[:, 0:128], rhs=zeros[:], start=True, stop=True)

        ident_bf = held.tile([128, 128], BF16, name="ident_bf")
        make_identity(nc, ident_bf[:])
        ident_f = held.tile([128, 128], F32, name="ident_f")
        make_identity(nc, ident_f[:])

        q_own = [held.tile([128, PAIRS, 2, N], BF16, name=f"q_own{x}") for x in range(2)]
        own = [slice(64 * x, 64 * (x + 1)) for x in range(2)]
        for x in range(2):
            nc.vector.memset(q_own[x][own[1 - x], 0, :, :], 0.0)
            nc.vector.tensor_copy(q_own[x][own[x], 0, :, :], q_sb[own[x], 0, :, :])
        for x in range(2):
            nc.gpsimd.memset(q_own[x][own[1 - x], 1:PAIRS, :, :], 0.0)
        for j in range(1, PAIRS):
            for x in range(2):
                nc.gpsimd.tensor_scalar(
                    q_own[x][own[x], j, :, :], q_sb[own[x], j, :, :], 1.0, 0.0, ALU.mult, ALU.add
                )

        scratch = held.tile([128, 1], F32, name="scratch")
        nc.vector.memset(scratch[:], 0.0)
        nc.scalar.activation(scratch[:], scratch[:], ACT.Exp)

        mask_term = held.tile([N, LK], BF16, name="mask_term")
        nc.vector.tensor_scalar(mask_term[:], mask_sb[:], -MASKED, MASKED, ALU.mult, ALU.add)

        ctx = [held.tile([DK, N], F32, name=f"ctx{h}") for h in range(H)]
        for h in range(H):
            if h == 1:
                bo_ps = psum_products.tile([DK, H], F32, name="bo_ps", tag="products")
                nc.tensor.matmul(bo_ps[:], lhsT=bo_rows[:], rhs=ident_f[0:H, 0:H], start=True, stop=True)
                bo_columns = held.tile([DK, H], F32, name="bo_columns")
                nc.scalar.copy(bo_columns[:], bo_ps[:])

            products = psum_products.tile([N, LK], F32)
            nc.tensor.matmul(products[:], lhsT=ident_bf[:], rhs=mask_term[:], start=True, stop=False)
            j, x = divmod(h, 2)
            for two in range(2):
                nc.tensor.matmul(
                    products[:], lhsT=q_own[x][:, j, two, :], rhs=k_sb[:, j, two, :], start=False, stop=(two == 1)
                )

            scores = work.tile([N, LK], F32)
            nc.vector.scalar_tensor_tensor(
                scores[:], products[:], 1.0 / math.sqrt(DK), bias_sb[:, h, :], ALU.mult, ALU.add
            )
            minus_top = work.tile([N, 1], F32)
            nc.vector.reduce_max(minus_top[:], scores[:], axis=mybir.AxisListType.X, negate=True)
            weights = work.tile([N, LK], BF16)
            total = work.tile([N, 1], F32)
            nc.scalar.activation(weights[:], scores[:], ACT.Exp, bias=minus_top[:], accum_out=total[:])
            inverse = work.tile([N, 1], F32)
            nc.vector.reciprocal(inverse[:], total[:])

            flipped_ps = psum_flip.tile([128, KEY_BLOCKS, N], BF16)
            for c in range(KEY_BLOCKS):
                nc.tensor.matmul(
                    flipped_ps[:, c, :], lhsT=weights[:, c * 128 : (c + 1) * 128], rhs=ident_bf[:], start=True, stop=True
                )
            flipped = work.tile([128, KEY_BLOCKS, N], BF16)
            nc.scalar.copy(flipped[:], flipped_ps[:])

            rows_ps = psum_rows.tile([N, DK], F32)
            for c in range(KEY_BLOCKS):
                nc.tensor.matmul(
                    rows_ps[:],
                    lhsT=flipped[:, c, :],
                    rhs=v_sb[:, c, h * DK : (h + 1) * DK],
                    start=(c == 0),
                    stop=(c == KEY_BLOCKS - 1),
                )
            rows = work.tile([N, DK], F32)
            nc.scalar.activation(rows[:], rows_ps[:], ACT.Copy, scale=inverse[:])
            ctx_ps = psum_ctx.tile([DK, N], F32)
            nc.tensor.transpose(ctx_ps[:], rows[:], ident_f[:])
            nc.scalar.copy(ctx[h][:], ctx_ps[:])

        bo_wide = held.tile([DK, H, N], F32, name="bo_wide")
        for h in range(H):
            if h % 2 == 0:
                two = slice(h, h + 2)
                nc.scalar.copy(bo_wide[:, two, :], bo_columns[:, two].unsqueeze(2).to_broadcast([DK, 2, N]))
            nc.vector.tensor_tensor(windows[h][:].indirect(offsets[:]), ctx[h][:], bo_wide[:, h, :], ALU.add)
            nc.sync.dma_start(out[h * DK : (h + 1) * DK, :], windows[h][:])
